import numpy as np
import ml_dtypes


def mxq(x, axis, fmt="e4m3"):
    dtype, down = {"e4m3": (ml_dtypes.float8_e4m3fn, 7), "e5m2": (ml_dtypes.float8_e5m2, 14)}[fmt]
    v = np.moveaxis(np.asarray(x, np.float32).astype(ml_dtypes.bfloat16).astype(np.float64), axis, -1)
    blocks = v.reshape(v.shape[:-1] + (-1, 32))
    amax = np.abs(blocks).max(-1, keepdims=True)
    byte = np.maximum(np.where(amax > 0, np.frexp(amax)[1] - 1 + 127, 0) - down, 1)
    scale = np.exp2(byte - 127.0)
    codes = (blocks / scale).astype(np.float32).astype(dtype).astype(np.float64)
    return np.moveaxis((codes * scale).reshape(v.shape), -1, axis)


WIDE = False


def mx_kscale(k):
    if not WIDE:
        return np.ones(k)
    levels = np.array([10, -10, 5, -5, 0])
    a = np.random.permutation(np.resize(levels, k // 512 * 4)).reshape(k // 512, 4)
    idx = np.arange(k)
    return np.exp2(a[idx // 512, idx % 128 // 32])


BF16 = ml_dtypes.bfloat16


def bf(x):
    return np.asarray(x, np.float32).astype(BF16)


def f64(x):
    return np.asarray(x).astype(np.float64)


B, C, D, DV, H, W = 1, 16384, 128, 256, 32, 16
N = H * W
HP, WP = H // 2, W // 2
M = HP * WP


def maxpool2(t):
    return t.reshape(B, t.shape[1], HP, 2, WP, 2).max(axis=(3, 5))


def setup_inputs():
    s = mx_kscale(C)
    return {"x": bf(np.random.standard_normal((B, C, H, W)) * s[None, :, None, None]),
            "Wq": bf(np.random.standard_normal((D, C)) * 0.5 / np.sqrt(C) / s[None, :]),
            "Wk": bf(np.random.standard_normal((D, C)) * 0.5 / np.sqrt(C) / s[None, :]),
            "Wv": bf(np.random.standard_normal((DV, C)) / np.sqrt(C) / s[None, :])}


def reference(x, Wq, Wk, Wv):
    xq = mxq(f64(x).reshape(B, C, N), 1, "e4m3")
    q = (mxq(f64(Wq), 1, "e4m3") @ xq).transpose(0, 2, 1)
    k = maxpool2((mxq(f64(Wk), 1, "e4m3") @ xq).reshape(B, D, H, W)).reshape(B, D, M)
    v = maxpool2((mxq(f64(Wv), 1, "e4m3") @ xq).reshape(B, DV, H, W)).reshape(B, DV, M)
    return q, k, v

@@ -1,0 +1,163 @@
+from contextlib import ExitStack
+
+import concourse.mybir as mybir
+from concourse.masks import make_identity
+
+F32 = mybir.dt.float32
+BF16 = mybir.dt.bfloat16
+U32 = mybir.dt.uint32
+U8 = mybir.dt.uint8
+FP8X4 = mybir.dt.float8_e4m3fn_x4
+
+P = 128
+PACK = 4
+K_PASS = P * PACK
+CHANNELS = 16384
+POSITIONS = 512
+ROW_TILES = 4
+PASSES = CHANNELS // K_PASS
+W_CHUNK_PASSES = 4
+W_CHUNK = W_CHUNK_PASSES * K_PASS
+W_LOADS = ROW_TILES * PASSES // W_CHUNK_PASSES
+W_LEAD = 6
+X_BUFS = 8
+W_BUFS = X_BUFS + W_LEAD + 2
+X_COLS_VECTOR = 320
+
+FLOPS = 2 * ROW_TILES * P * CHANNELS * POSITIONS
+
+
+def tile_selfattention_pa_k_kernel(tc, x, Wq, Wk, Wv, out_0, out_1, out_2):
+    nc = tc.nc
+    x_rows = x.rearrange("b c h w -> (b c) (h w)")
+    w_rows = [Wq, Wk, Wv[0:P, :], Wv[P : 2 * P, :]]
+
+    with ExitStack() as ctx:
+        ctx.enter_context(tc.manual_schedule())
+        consts = ctx.enter_context(tc.tile_pool(name="consts", bufs=1))
+        x_pool = ctx.enter_context(tc.tile_pool(name="x_pool", bufs=X_BUFS))
+        w_pool = ctx.enter_context(tc.tile_pool(name="w_pool", bufs=W_BUFS))
+        grouped = ctx.enter_context(tc.tile_pool(name="grouped", bufs=3))
+        packed = ctx.enter_context(tc.tile_pool(name="packed", bufs=3))
+        results = ctx.enter_context(tc.tile_pool(name="results", bufs=1))
+        acc_pool = ctx.enter_context(tc.psum_pool(name="acc_pool", bufs=1))
+        flip_pool = ctx.enter_context(tc.psum_pool(name="flip_pool", bufs=4))
+
+        ident = consts.tile([P, P], F32)
+        make_identity(nc, ident[:])
+
+        acc = [acc_pool.tile([P, POSITIONS], F32, name="acc%d" % a) for a in range(ROW_TILES)]
+
+        x_raw = {}
+        w_raw = {}
+        flipped = {}
+        w_grouped = {}
+
+        def load_w(j):
+            if j >= W_LOADS:
+                return
+            chunk, a = divmod(j, ROW_TILES)
+            raw_w = w_pool.tile([P, W_CHUNK], BF16)
+            nc.sync.dma_start(out=raw_w[:], in_=w_rows[a][:, chunk * W_CHUNK : (chunk + 1) * W_CHUNK])
+            w_raw[(chunk, a)] = raw_w
+
+        def load_x(g):
+            if g >= PASSES:
+                return
+            raw_x = x_pool.tile([P, PACK, POSITIONS], BF16)
+            nc.sync.dma_start(
+                out=raw_x[:].rearrange("p (u e) n -> p u (e n)", u=2),
+                in_=x_rows[g * K_PASS : (g + 1) * K_PASS, :].rearrange("(u q e) n -> q u (e n)", u=2, e=2),
+            )
+            x_raw[g] = raw_x
+
+        def flip_w(g):
+            chunk, g_in = divmod(g, W_CHUNK_PASSES)
+            for half in range(2):
+                bank = flip_pool.tile([P, 2, 2, P], F32)
+                for a2 in range(2):
+                    words = w_raw[(chunk, 2 * half + a2)][:].bitcast(F32)
+                    for u in range(2):
+                        first = g_in * (K_PASS // 2) + u * P
+                        nc.tensor.transpose(bank[:, a2, u, :], words[:, first : first + P], ident[:])
+                flipped[(g, half)] = bank
+
+        def copy_w(g):
+            group_w = grouped.tile([P, ROW_TILES * P * PACK], BF16, align_bytes=64)
+            words = group_w[:].bitcast(F32).rearrange("p (a r u) -> p a r u", a=ROW_TILES, u=2)
+            for half in range(2):
+                nc.scalar.copy(
+                    out=words[:, 2 * half : 2 * half + 2, :, :],
+                    in_=flipped[(g, half)][:].rearrange("p a u r -> p a r u"),
+                )
+            w_grouped[g] = group_w
+
+        def regroup_x(g):
+            group_x = grouped.tile([P, POSITIONS, PACK], BF16, align_bytes=64)
+            cut = X_COLS_VECTOR
+            nc.vector.tensor_copy(
+                out=group_x[:, 0:cut, :].rearrange("p (c i) t -> p c t i", i=4),
+                in_=x_raw[g][:, :, 0:cut].rearrange("p t (c i) -> p c t i", i=4),
+            )
+            nc.scalar.copy(
+                out=group_x[:, cut:POSITIONS, :].rearrange("p (c i) t -> p c t i", i=4),
+                in_=x_raw[g][:, :, cut:POSITIONS].rearrange("p t (c i) -> p c t i", i=4),
+            )
+            return group_x
+
+        def quantise(values, label):
+            codes = packed.tile([P, POSITIONS], U32, align_bytes=64, name="codes_" + label)
+            scales = packed.tile([P, POSITIONS], U8, align_bytes=64, name="scales_" + label)
+            nc.vector.quantize_mx(out=codes[:].bitcast(FP8X4), scales=scales[:], in_=values)
+            return codes, scales
+
+        for j in range(W_LEAD):
+            load_w(j)
+        for g in range(X_BUFS):
+            load_x(g)
+            load_w(g + W_LEAD)
+
+        for step in range(PASSES + 2):
+            g = step - 2
+            if step < PASSES:
+                flip_w(step)
+            if g >= 0:
+                group_x = regroup_x(g)
+            if 1 <= step <= PASSES:
+                copy_w(step - 1)
+            if g >= 0:
+                w_codes, w_scales = quantise(w_grouped[g][:], "w")
+                x_codes, x_scales = quantise(group_x[:].rearrange("p n t -> p (n t)"), "x")
+                for a in range(ROW_TILES):
+                    rows = slice(a * P, (a + 1) * P)
+                    nc.tensor.matmul_mx(
+                        out=acc[a][:],
+                        lhsT=w_codes[:, rows].bitcast(FP8X4),
+                        lhsT_scale=w_scales[:, rows],
+                        rhs=x_codes[:].bitcast(FP8X4),
+                        rhs_scale=x_scales[:],
+                        start=(g == 0),
+                        stop=(g == PASSES - 1),
+                    )
+                load_x(g + X_BUFS)
+                load_w(g + X_BUFS + W_LEAD)
+
+        q_sb = results.tile([P, POSITIONS], F32)
+        nc.scalar.copy(out=q_sb[:], in_=acc[0][:])
+        q_flip = flip_pool.tile([P, 4, P], F32, name="bank")
+        for b in range(4):
+            nc.tensor.transpose(q_flip[:, b, :], q_sb[:, b * P : (b + 1) * P], ident[:])
+        q_out = results.tile([P, 4, P], F32)
+        nc.scalar.copy(out=q_out[:], in_=q_flip[:])
+        nc.sync.dma_start(out=out_0[0].rearrange("(b p) d -> p b d", p=P), in_=q_out[:])
+
+        pooled_dst = [out_1[0], out_2[0][0:P, :], out_2[0][P : 2 * P, :]]
+        for a in range(1, ROW_TILES):
+            pooled = results.tile([P, 16, 8], F32, name="pooled%d" % a)
+            nc.vector.tensor_reduce(
+                out=pooled[:],
+                in_=acc[a][:].rearrange("p (hp i wp j) -> p hp wp i j", hp=16, i=2, wp=8, j=2),
+                axis=mybir.AxisListType.XY,
+                op=mybir.AluOpType.max,
+            )
+            nc.sync.dma_start(out=pooled_dst[a - 1], in_=pooled[:].rearrange("p hp wp -> p (hp wp)"))

@@ -16,12 +16,15 @@ CHANNELS = 16384
 POSITIONS = 512
 ROW_TILES = 4
 PASSES = CHANNELS // K_PASS
-W_CHUNK_PASSES = 4
-W_CHUNK = W_CHUNK_PASSES * K_PASS
-W_LOADS = ROW_TILES * PASSES // W_CHUNK_PASSES
-W_LEAD = 6
+CHUNK_PASSES = 4
+CHUNK = CHUNK_PASSES * K_PASS
+STEPS = PASSES
+W_LEAD = 2
+FLIP_AHEAD = 2
+COPY_AHEAD = 1
 X_BUFS = 8
-W_BUFS = X_BUFS + W_LEAD + 2
+W_BUFS = X_BUFS + W_LEAD
+PACKED_BUFS = 2 * CHUNK_PASSES
 X_COLS_VECTOR = 320
 
 FLOPS = 2 * ROW_TILES * P * CHANNELS * POSITIONS
@@ -38,7 +41,7 @@ def tile_selfattention_pa_k_kernel(tc, x, Wq, Wk, Wv, out_0, out_1, out_2):
         x_pool = ctx.enter_context(tc.tile_pool(name="x_pool", bufs=X_BUFS))
         w_pool = ctx.enter_context(tc.tile_pool(name="w_pool", bufs=W_BUFS))
         grouped = ctx.enter_context(tc.tile_pool(name="grouped", bufs=3))
-        packed = ctx.enter_context(tc.tile_pool(name="packed", bufs=3))
+        packed = ctx.enter_context(tc.tile_pool(name="packed", bufs=PACKED_BUFS))
         results = ctx.enter_context(tc.tile_pool(name="results", bufs=1))
         acc_pool = ctx.enter_context(tc.psum_pool(name="acc_pool", bufs=1))
         flip_pool = ctx.enter_context(tc.psum_pool(name="flip_pool", bufs=4))
@@ -52,56 +55,57 @@ def tile_selfattention_pa_k_kernel(tc, x, Wq, Wk, Wv, out_0, out_1, out_2):
         w_raw = {}
         flipped = {}
         w_grouped = {}
+        w_packed = {}
+        x_packed = {}
 
-        def load_w(j):
-            if j >= W_LOADS:
+        def load_w(s):
+            if s >= STEPS:
                 return
-            chunk, a = divmod(j, ROW_TILES)
-            raw_w = w_pool.tile([P, W_CHUNK], BF16)
-            nc.sync.dma_start(out=raw_w[:], in_=w_rows[a][:, chunk * W_CHUNK : (chunk + 1) * W_CHUNK])
-            w_raw[(chunk, a)] = raw_w
+            chunk, a = divmod(s, ROW_TILES)
+            raw_w = w_pool.tile([P, CHUNK], BF16)
+            nc.sync.dma_start(out=raw_w[:], in_=w_rows[a][:, chunk * CHUNK : (chunk + 1) * CHUNK])
+            w_raw[s] = raw_w
 
-        def load_x(g):
-            if g >= PASSES:
+        def load_x(s):
+            if s >= STEPS:
                 return
             raw_x = x_pool.tile([P, PACK, POSITIONS], BF16)
             nc.sync.dma_start(
                 out=raw_x[:].rearrange("p (u e) n -> p u (e n)", u=2),
-                in_=x_rows[g * K_PASS : (g + 1) * K_PASS, :].rearrange("(u q e) n -> q u (e n)", u=2, e=2),
+                in_=x_rows[s * K_PASS : (s + 1) * K_PASS, :].rearrange("(u q e) n -> q u (e n)", u=2, e=2),
             )
-            x_raw[g] = raw_x
+            x_raw[s] = raw_x
 
-        def flip_w(g):
-            chunk, g_in = divmod(g, W_CHUNK_PASSES)
+        def flip_w(s):
+            words = w_raw[s][:].bitcast(F32)
             for half in range(2):
                 bank = flip_pool.tile([P, 2, 2, P], F32)
-                for a2 in range(2):
-                    words = w_raw[(chunk, 2 * half + a2)][:].bitcast(F32)
+                for g2 in range(2):
                     for u in range(2):
-                        first = g_in * (K_PASS // 2) + u * P
-                        nc.tensor.transpose(bank[:, a2, u, :], words[:, first : first + P], ident[:])
-                flipped[(g, half)] = bank
+                        first = (2 * half + g2) * (K_PASS // 2) + u * P
+                        nc.tensor.transpose(bank[:, g2, u, :], words[:, first : first + P], ident[:])
+                flipped[(s, half)] = bank
 
-        def copy_w(g):
-            group_w = grouped.tile([P, ROW_TILES * P * PACK], BF16, align_bytes=64)
-            words = group_w[:].bitcast(F32).rearrange("p (a r u) -> p a r u", a=ROW_TILES, u=2)
+        def copy_w(s):
+            group_w = grouped.tile([P, CHUNK_PASSES * P * PACK], BF16, align_bytes=64)
+            words = group_w[:].bitcast(F32).rearrange("p (g r u) -> p g r u", g=CHUNK_PASSES, u=2)
             for half in range(2):
                 nc.scalar.copy(
                     out=words[:, 2 * half : 2 * half + 2, :, :],
-                    in_=flipped[(g, half)][:].rearrange("p a u r -> p a r u"),
+                    in_=flipped[(s, half)][:].rearrange("p g u r -> p g r u"),
                 )
-            w_grouped[g] = group_w
+            w_grouped[s] = group_w
 
-        def regroup_x(g):
+        def regroup_x(s):
             group_x = grouped.tile([P, POSITIONS, PACK], BF16, align_bytes=64)
             cut = X_COLS_VECTOR
             nc.vector.tensor_copy(
                 out=group_x[:, 0:cut, :].rearrange("p (c i) t -> p c t i", i=4),
-                in_=x_raw[g][:, :, 0:cut].rearrange("p t (c i) -> p c t i", i=4),
+                in_=x_raw[s][:, :, 0:cut].rearrange("p t (c i) -> p c t i", i=4),
             )
             nc.scalar.copy(
                 out=group_x[:, cut:POSITIONS, :].rearrange("p (c i) t -> p c t i", i=4),
-                in_=x_raw[g][:, :, cut:POSITIONS].rearrange("p t (c i) -> p c t i", i=4),
+                in_=x_raw[s][:, :, cut:POSITIONS].rearrange("p t (c i) -> p c t i", i=4),
             )
             return group_x
 
@@ -111,36 +115,44 @@ def tile_selfattention_pa_k_kernel(tc, x, Wq, Wk, Wv, out_0, out_1, out_2):
             nc.vector.quantize_mx(out=codes[:].bitcast(FP8X4), scales=scales[:], in_=values)
             return codes, scales
 
-        for j in range(W_LEAD):
-            load_w(j)
-        for g in range(X_BUFS):
-            load_x(g)
-            load_w(g + W_LEAD)
+        def multiply(g, a):
+            chunk, g_in = divmod(g, CHUNK_PASSES)
+            w_codes, w_scales = w_packed[chunk * ROW_TILES + a]
+            x_codes, x_scales = x_packed[g]
+            rows = slice(g_in * P, (g_in + 1) * P)
+            nc.tensor.matmul_mx(
+                out=acc[a][:],
+                lhsT=w_codes[:, rows].bitcast(FP8X4),
+                lhsT_scale=w_scales[:, rows],
+                rhs=x_codes[:].bitcast(FP8X4),
+                rhs_scale=x_scales[:],
+                start=(g == 0),
+                stop=(g == PASSES - 1),
+            )
 
-        for step in range(PASSES + 2):
-            g = step - 2
-            if step < PASSES:
-                flip_w(step)
-            if g >= 0:
-                group_x = regroup_x(g)
-            if 1 <= step <= PASSES:
-                copy_w(step - 1)
-            if g >= 0:
-                w_codes, w_scales = quantise(w_grouped[g][:], "w")
-                x_codes, x_scales = quantise(group_x[:].rearrange("p n t -> p (n t)"), "x")
-                for a in range(ROW_TILES):
-                    rows = slice(a * P, (a + 1) * P)
-                    nc.tensor.matmul_mx(
-                        out=acc[a][:],
-                        lhsT=w_codes[:, rows].bitcast(FP8X4),
-                        lhsT_scale=w_scales[:, rows],
-                        rhs=x_codes[:].bitcast(FP8X4),
-                        rhs_scale=x_scales[:],
-                        start=(g == 0),
-                        stop=(g == PASSES - 1),
-                    )
-                load_x(g + X_BUFS)
-                load_w(g + X_BUFS + W_LEAD)
+        for s in range(W_LEAD):
+            load_w(s)
+        for s in range(X_BUFS):
+            load_x(s)
+            load_w(s + W_LEAD)
+
+        for s in range(-FLIP_AHEAD, STEPS):
+            if s + FLIP_AHEAD < STEPS:
+                flip_w(s + FLIP_AHEAD)
+            if s >= 0:
+                group_x = regroup_x(s)
+            if 0 <= s + COPY_AHEAD < STEPS:
+                copy_w(s + COPY_AHEAD)
+            if s >= 0:
+                w_packed[s] = quantise(w_grouped[s][:], "w")
+                x_packed[s] = quantise(group_x[:].rearrange("p n t -> p (n t)"), "x")
+                first = s - s % CHUNK_PASSES
+                for g in range(first, s):
+                    multiply(g, s - first)
+                for a in range(s - first + 1):
+                    multiply(s, a)
+                load_x(s + X_BUFS)
+                load_w(s + X_BUFS + W_LEAD)
 
         q_sb = results.tile([P, POSITIONS], F32)
         nc.scalar.copy(out=q_sb[:], in_=acc[0][:])

@@ -19,7 +19,7 @@ PASSES = CHANNELS // K_PASS
 CHUNK_PASSES = 4
 CHUNK = CHUNK_PASSES * K_PASS
 STEPS = PASSES
-W_LEAD = 2
+W_LEAD = 1
 FLIP_AHEAD = 2
 COPY_AHEAD = 1
 X_BUFS = 8
@@ -154,22 +154,29 @@ def tile_selfattention_pa_k_kernel(tc, x, Wq, Wk, Wv, out_0, out_1, out_2):
                 load_x(s + X_BUFS)
                 load_w(s + X_BUFS + W_LEAD)
 
+        def pool_2x2(pooled, a):
+            nc.vector.tensor_reduce(
+                out=pooled,
+                in_=acc[a][:].rearrange("p (hp i wp j) -> p hp wp i j", hp=16, i=2, wp=8, j=2),
+                axis=mybir.AxisListType.XY,
+                op=mybir.AluOpType.max,
+            )
+
         q_sb = results.tile([P, POSITIONS], F32)
         nc.scalar.copy(out=q_sb[:], in_=acc[0][:])
+        k_pooled = results.tile([P, 16, 8], F32)
+        pool_2x2(k_pooled[:], 1)
+        nc.sync.dma_start(out=out_1[0], in_=k_pooled[:].rearrange("p hp wp -> p (hp wp)"))
         q_flip = flip_pool.tile([P, 4, P], F32, name="bank")
         for b in range(4):
             nc.tensor.transpose(q_flip[:, b, :], q_sb[:, b * P : (b + 1) * P], ident[:])
         q_out = results.tile([P, 4, P], F32)
         nc.scalar.copy(out=q_out[:], in_=q_flip[:])
         nc.sync.dma_start(out=out_0[0].rearrange("(b p) d -> p b d", p=P), in_=q_out[:])
-
-        pooled_dst = [out_1[0], out_2[0][0:P, :], out_2[0][P : 2 * P, :]]
-        for a in range(1, ROW_TILES):
-            pooled = results.tile([P, 16, 8], F32, name="pooled%d" % a)
-            nc.vector.tensor_reduce(
-                out=pooled[:],
-                in_=acc[a][:].rearrange("p (hp i wp j) -> p hp wp i j", hp=16, i=2, wp=8, j=2),
-                axis=mybir.AxisListType.XY,
-                op=mybir.AluOpType.max,
-            )
-            nc.sync.dma_start(out=pooled_dst[a - 1], in_=pooled[:].rearrange("p hp wp -> p (hp wp)"))
+        v_pooled = results.tile([P, 2, 16, 8], F32)
+        pool_2x2(v_pooled[:, 0, :, :], 2)
+        pool_2x2(v_pooled[:, 1, :, :], 3)
+        nc.sync.dma_start(
+            out=out_2[0].rearrange("(a p) m -> p a m", p=P),
+            in_=v_pooled[:].rearrange("p a hp wp -> p a (hp wp)"),
+        )

@@ -16,15 +16,17 @@ CHANNELS = 16384
 POSITIONS = 512
 ROW_TILES = 4
 PASSES = CHANNELS // K_PASS
-CHUNK_PASSES = 4
-CHUNK = CHUNK_PASSES * K_PASS
+UNIT_PASSES = 4
+UNIT = UNIT_PASSES * K_PASS
+PERIODS = (4, 8, 8, 8, 4)
 STEPS = PASSES
 W_LEAD = 1
 FLIP_AHEAD = 2
 COPY_AHEAD = 1
+RUN_LIMIT = 5
 X_BUFS = 8
-W_BUFS = X_BUFS + W_LEAD
-PACKED_BUFS = 2 * CHUNK_PASSES
+W_BUFS = 8
+PACKED_BUFS = 2 * max(PERIODS) + 2
 X_COLS_VECTOR = 320
 
 FLOPS = 2 * ROW_TILES * P * CHANNELS * POSITIONS
@@ -58,13 +60,28 @@ def tile_selfattention_pa_k_kernel(tc, x, Wq, Wk, Wv, out_0, out_1, out_2):
         w_packed = {}
         x_packed = {}
 
+        unit_at = []
+        w_loads = {}
+        start = 0
+        for passes in PERIODS:
+            for a in range(ROW_TILES):
+                w_loads[len(unit_at)] = (a, start, passes)
+                for first in range(start, start + passes, UNIT_PASSES):
+                    unit_at.append((a, first))
+            start += passes
+        unit_step = dict((unit_at[s], s) for s in range(STEPS))
+
         def load_w(s):
-            if s >= STEPS:
+            if s not in w_loads:
                 return
-            chunk, a = divmod(s, ROW_TILES)
-            raw_w = w_pool.tile([P, CHUNK], BF16)
-            nc.sync.dma_start(out=raw_w[:], in_=w_rows[a][:, chunk * CHUNK : (chunk + 1) * CHUNK])
-            w_raw[s] = raw_w
+            a, first, passes = w_loads[s]
+            raw_w = w_pool.tile([P, max(PERIODS) * K_PASS], BF16)
+            nc.sync.dma_start(
+                out=raw_w[:, 0 : passes * K_PASS],
+                in_=w_rows[a][:, first * K_PASS : (first + passes) * K_PASS],
+            )
+            for h in range(passes // UNIT_PASSES):
+                w_raw[s + h] = raw_w[:, h * UNIT : (h + 1) * UNIT]
 
         def load_x(s):
             if s >= STEPS:
@@ -77,7 +94,7 @@ def tile_selfattention_pa_k_kernel(tc, x, Wq, Wk, Wv, out_0, out_1, out_2):
             x_raw[s] = raw_x
 
         def flip_w(s):
-            words = w_raw[s][:].bitcast(F32)
+            words = w_raw[s].bitcast(F32)
             for half in range(2):
                 bank = flip_pool.tile([P, 2, 2, P], F32)
                 for g2 in range(2):
@@ -87,8 +104,8 @@ def tile_selfattention_pa_k_kernel(tc, x, Wq, Wk, Wv, out_0, out_1, out_2):
                 flipped[(s, half)] = bank
 
         def copy_w(s):
-            group_w = grouped.tile([P, CHUNK_PASSES * P * PACK], BF16, align_bytes=64)
-            words = group_w[:].bitcast(F32).rearrange("p (g r u) -> p g r u", g=CHUNK_PASSES, u=2)
+            group_w = grouped.tile([P, UNIT_PASSES * P * PACK], BF16, align_bytes=64)
+            words = group_w[:].bitcast(F32).rearrange("p (g r u) -> p g r u", g=UNIT_PASSES, u=2)
             for half in range(2):
                 nc.scalar.copy(
                     out=words[:, 2 * half : 2 * half + 2, :, :],
@@ -116,8 +133,8 @@ def tile_selfattention_pa_k_kernel(tc, x, Wq, Wk, Wv, out_0, out_1, out_2):
             return codes, scales
 
         def multiply(g, a):
-            chunk, g_in = divmod(g, CHUNK_PASSES)
-            w_codes, w_scales = w_packed[chunk * ROW_TILES + a]
+            g_in = g % UNIT_PASSES
+            w_codes, w_scales = w_packed[unit_step[(a, g - g_in)]]
             x_codes, x_scales = x_packed[g]
             rows = slice(g_in * P, (g_in + 1) * P)
             nc.tensor.matmul_mx(
@@ -136,6 +153,7 @@ def tile_selfattention_pa_k_kernel(tc, x, Wq, Wk, Wv, out_0, out_1, out_2):
             load_x(s)
             load_w(s + W_LEAD)
 
+        waiting = []
         for s in range(-FLIP_AHEAD, STEPS):
             if s + FLIP_AHEAD < STEPS:
                 flip_w(s + FLIP_AHEAD)
@@ -146,11 +164,13 @@ def tile_selfattention_pa_k_kernel(tc, x, Wq, Wk, Wv, out_0, out_1, out_2):
             if s >= 0:
                 w_packed[s] = quantise(w_grouped[s][:], "w")
                 x_packed[s] = quantise(group_x[:].rearrange("p n t -> p (n t)"), "x")
-                first = s - s % CHUNK_PASSES
-                for g in range(first, s):
-                    multiply(g, s - first)
-                for a in range(s - first + 1):
-                    multiply(s, a)
+                a_new, first = unit_at[s]
+                waiting.extend([(g, a_new) for g in range(first, min(first + UNIT_PASSES, s))])
+                waiting.extend([(s, a) for a in range(ROW_TILES) if unit_step[(a, s - s % UNIT_PASSES)] <= s])
+                count = len(waiting) if s >= STEPS - PERIODS[-1] else min(RUN_LIMIT, len(waiting))
+                for g, a in waiting[0:count]:
+                    multiply(g, a)
+                waiting = waiting[count:]
                 load_x(s + X_BUFS)
                 load_w(s + X_BUFS + W_LEAD)
 

@@ -35,7 +35,8 @@ FLOPS = 2 * ROW_TILES * P * CHANNELS * POSITIONS
 def tile_selfattention_pa_k_kernel(tc, x, Wq, Wk, Wv, out_0, out_1, out_2):
     nc = tc.nc
     x_rows = x.rearrange("b c h w -> (b c) (h w)")
-    w_rows = [Wq, Wk, Wv[0:P, :], Wv[P : 2 * P, :]]
+    wv_rows = Wv.rearrange("(p a) k -> a p k", a=2)
+    w_rows = [Wq, Wk, wv_rows[0], wv_rows[1]]
 
     with ExitStack() as ctx:
         ctx.enter_context(tc.manual_schedule())
@@ -183,7 +184,9 @@ def tile_selfattention_pa_k_kernel(tc, x, Wq, Wk, Wv, out_0, out_1, out_2):
             )
 
         q_sb = results.tile([P, POSITIONS], F32)
-        nc.scalar.copy(out=q_sb[:], in_=acc[0][:])
+        nc.scalar.copy(
+            out=q_sb[:].rearrange("d (i p) -> d i p", i=4), in_=acc[0][:].rearrange("d (p i) -> d i p", i=4)
+        )
         k_pooled = results.tile([P, 16, 8], F32)
         pool_2x2(k_pooled[:], 1)
         nc.sync.dma_start(out=out_1[0], in_=k_pooled[:].rearrange("p hp wp -> p (hp wp)"))
@@ -192,11 +195,13 @@ def tile_selfattention_pa_k_kernel(tc, x, Wq, Wk, Wv, out_0, out_1, out_2):
             nc.tensor.transpose(q_flip[:, b, :], q_sb[:, b * P : (b + 1) * P], ident[:])
         q_out = results.tile([P, 4, P], F32)
         nc.scalar.copy(out=q_out[:], in_=q_flip[:])
-        nc.sync.dma_start(out=out_0[0].rearrange("(b p) d -> p b d", p=P), in_=q_out[:])
+        nc.sync.dma_start(
+            out=out_0[0].rearrange("(p i) d -> p (i d)", i=4), in_=q_out[:].rearrange("p i d -> p (i d)")
+        )
         v_pooled = results.tile([P, 2, 16, 8], F32)
         pool_2x2(v_pooled[:, 0, :, :], 2)
         pool_2x2(v_pooled[:, 1, :, :], 3)
         nc.sync.dma_start(
-            out=out_2[0].rearrange("(a p) m -> p a m", p=P),
-            in_=v_pooled[:].rearrange("p a hp wp -> p a (hp wp)"),
+            out=out_2[0].rearrange("(p a) m -> p (a m)", a=2),
+            in_=v_pooled[:].rearrange("p a hp wp -> p (a hp wp)"),
         )

@@ -24,6 +24,8 @@ W_LEAD = 1
 FLIP_AHEAD = 2
 COPY_AHEAD = 1
 RUN_LIMIT = 5
+CONSECUTIVE_FROM = 0
+CONSECUTIVE_TO = 32
 X_BUFS = 8
 W_BUFS = 8
 PACKED_BUFS = 2 * max(PERIODS) + 2
@@ -84,14 +86,23 @@ def tile_selfattention_pa_k_kernel(tc, x, Wq, Wk, Wv, out_0, out_1, out_2):
             for h in range(passes // UNIT_PASSES):
                 w_raw[s + h] = raw_w[:, h * UNIT : (h + 1) * UNIT]
 
+        def consecutive(g):
+            return CONSECUTIVE_FROM <= g < CONSECUTIVE_TO
+
         def load_x(s):
             if s >= STEPS:
                 return
             raw_x = x_pool.tile([P, PACK, POSITIONS], BF16)
-            nc.sync.dma_start(
-                out=raw_x[:].rearrange("p (u e) n -> p u (e n)", u=2),
-                in_=x_rows[s * K_PASS : (s + 1) * K_PASS, :].rearrange("(u q e) n -> q u (e n)", u=2, e=2),
-            )
+            if consecutive(s):
+                nc.sync.dma_start(
+                    out=raw_x[:].rearrange("p t n -> p (t n)"),
+                    in_=x_rows[s * K_PASS : (s + 1) * K_PASS, :].rearrange("(q t) n -> q (t n)", t=PACK),
+                )
+            else:
+                nc.sync.dma_start(
+                    out=raw_x[:].rearrange("p (u e) n -> p u (e n)", u=2),
+                    in_=x_rows[s * K_PASS : (s + 1) * K_PASS, :].rearrange("(u q e) n -> q u (e n)", u=2, e=2),
+                )
             x_raw[s] = raw_x
 
         def flip_w(s):
@@ -100,8 +111,12 @@ def tile_selfattention_pa_k_kernel(tc, x, Wq, Wk, Wv, out_0, out_1, out_2):
                 bank = flip_pool.tile([P, 2, 2, P], F32)
                 for g2 in range(2):
                     for u in range(2):
-                        first = (2 * half + g2) * (K_PASS // 2) + u * P
-                        nc.tensor.transpose(bank[:, g2, u, :], words[:, first : first + P], ident[:])
+                        first = (2 * half + g2) * (K_PASS // 2)
+                        if consecutive(unit_at[s][1]):
+                            picked = words[:, first + u : first + 2 * P : 2]
+                        else:
+                            picked = words[:, first + u * P : first + (u + 1) * P]
+                        nc.tensor.transpose(bank[:, g2, u, :], picked, ident[:])
                 flipped[(s, half)] = bank
 
         def copy_w(s):

@@ -24,8 +24,6 @@ W_LEAD = 1
 FLIP_AHEAD = 2
 COPY_AHEAD = 1
 RUN_LIMIT = 5
-CONSECUTIVE_FROM = 0
-CONSECUTIVE_TO = 32
 X_BUFS = 8
 W_BUFS = 8
 PACKED_BUFS = 2 * max(PERIODS) + 2
@@ -87,7 +85,7 @@ def tile_selfattention_pa_k_kernel(tc, x, Wq, Wk, Wv, out_0, out_1, out_2):
                 w_raw[s + h] = raw_w[:, h * UNIT : (h + 1) * UNIT]
 
         def consecutive(g):
-            return CONSECUTIVE_FROM <= g < CONSECUTIVE_TO
+            return (g // UNIT_PASSES) % 4 != 3
 
         def load_x(s):
             if s >= STEPS:

from contextlib import ExitStack

import concourse.mybir as mybir
from concourse.masks import make_identity

F32 = mybir.dt.float32
BF16 = mybir.dt.bfloat16
U32 = mybir.dt.uint32
U8 = mybir.dt.uint8
FP8X4 = mybir.dt.float8_e4m3fn_x4

P = 128
PACK = 4
K_PASS = P * PACK
CHANNELS = 16384
POSITIONS = 512
ROW_TILES = 4
PASSES = CHANNELS // K_PASS
UNIT_PASSES = 4
UNIT = UNIT_PASSES * K_PASS
PERIODS = (4, 8, 8, 8, 4)
STEPS = PASSES
W_LEAD = 1
FLIP_AHEAD = 2
COPY_AHEAD = 1
RUN_LIMIT = 5
X_BUFS = 8
W_BUFS = 8
PACKED_BUFS = 2 * max(PERIODS) + 2
X_COLS_VECTOR = 320

FLOPS = 2 * ROW_TILES * P * CHANNELS * POSITIONS


def tile_selfattention_pa_k_kernel(tc, x, Wq, Wk, Wv, out_0, out_1, out_2):
    nc = tc.nc
    x_rows = x.rearrange("b c h w -> (b c) (h w)")
    wv_rows = Wv.rearrange("(p a) k -> a p k", a=2)
    w_rows = [Wq, Wk, wv_rows[0], wv_rows[1]]

    with ExitStack() as ctx:
        ctx.enter_context(tc.manual_schedule())
        consts = ctx.enter_context(tc.tile_pool(name="consts", bufs=1))
        x_pool = ctx.enter_context(tc.tile_pool(name="x_pool", bufs=X_BUFS))
        w_pool = ctx.enter_context(tc.tile_pool(name="w_pool", bufs=W_BUFS))
        grouped = ctx.enter_context(tc.tile_pool(name="grouped", bufs=3))
        packed = ctx.enter_context(tc.tile_pool(name="packed", bufs=PACKED_BUFS))
        results = ctx.enter_context(tc.tile_pool(name="results", bufs=1))
        acc_pool = ctx.enter_context(tc.psum_pool(name="acc_pool", bufs=1))
        flip_pool = ctx.enter_context(tc.psum_pool(name="flip_pool", bufs=4))

        ident = consts.tile([P, P], F32)
        make_identity(nc, ident[:])

        acc = [acc_pool.tile([P, POSITIONS], F32, name="acc%d" % a) for a in range(ROW_TILES)]

        x_raw = {}
        w_raw = {}
        flipped = {}
        w_grouped = {}
        w_packed = {}
        x_packed = {}

        unit_at = []
        w_loads = {}
        start = 0
        for passes in PERIODS:
            for a in range(ROW_TILES):
                w_loads[len(unit_at)] = (a, start, passes)
                for first in range(start, start + passes, UNIT_PASSES):
                    unit_at.append((a, first))
            start += passes
        unit_step = dict((unit_at[s], s) for s in range(STEPS))

        def load_w(s):
            if s not in w_loads:
                return
            a, first, passes = w_loads[s]
            raw_w = w_pool.tile([P, max(PERIODS) * K_PASS], BF16)
            nc.sync.dma_start(
                out=raw_w[:, 0 : passes * K_PASS],
                in_=w_rows[a][:, first * K_PASS : (first + passes) * K_PASS],
            )
            for h in range(passes // UNIT_PASSES):
                w_raw[s + h] = raw_w[:, h * UNIT : (h + 1) * UNIT]

        def consecutive(g):
            return (g // UNIT_PASSES) % 4 != 3

        def load_x(s):
            if s >= STEPS:
                return
            raw_x = x_pool.tile([P, PACK, POSITIONS], BF16)
            if consecutive(s):
                nc.sync.dma_start(
                    out=raw_x[:].rearrange("p t n -> p (t n)"),
                    in_=x_rows[s * K_PASS : (s + 1) * K_PASS, :].rearrange("(q t) n -> q (t n)", t=PACK),
                )
            else:
                nc.sync.dma_start(
                    out=raw_x[:].rearrange("p (u e) n -> p u (e n)", u=2),
                    in_=x_rows[s * K_PASS : (s + 1) * K_PASS, :].rearrange("(u q e) n -> q u (e n)", u=2, e=2),
                )
            x_raw[s] = raw_x

        def flip_w(s):
            words = w_raw[s].bitcast(F32)
            for half in range(2):
                bank = flip_pool.tile([P, 2, 2, P], F32)
                for g2 in range(2):
                    for u in range(2):
                        first = (2 * half + g2) * (K_PASS // 2)
                        if consecutive(unit_at[s][1]):
                            picked = words[:, first + u : first + 2 * P : 2]
                        else:
                            picked = words[:, first + u * P : first + (u + 1) * P]
                        nc.tensor.transpose(bank[:, g2, u, :], picked, ident[:])
                flipped[(s, half)] = bank

        def copy_w(s):
            group_w = grouped.tile([P, UNIT_PASSES * P * PACK], BF16, align_bytes=64)
            words = group_w[:].bitcast(F32).rearrange("p (g r u) -> p g r u", g=UNIT_PASSES, u=2)
            for half in range(2):
                nc.scalar.copy(
                    out=words[:, 2 * half : 2 * half + 2, :, :],
                    in_=flipped[(s, half)][:].rearrange("p g u r -> p g r u"),
                )
            w_grouped[s] = group_w

        def regroup_x(s):
            group_x = grouped.tile([P, POSITIONS, PACK], BF16, align_bytes=64)
            cut = X_COLS_VECTOR
            nc.vector.tensor_copy(
                out=group_x[:, 0:cut, :].rearrange("p (c i) t -> p c t i", i=4),
                in_=x_raw[s][:, :, 0:cut].rearrange("p t (c i) -> p c t i", i=4),
            )
            nc.scalar.copy(
                out=group_x[:, cut:POSITIONS, :].rearrange("p (c i) t -> p c t i", i=4),
                in_=x_raw[s][:, :, cut:POSITIONS].rearrange("p t (c i) -> p c t i", i=4),
            )
            return group_x

        def quantise(values, label):
            codes = packed.tile([P, POSITIONS], U32, align_bytes=64, name="codes_" + label)
            scales = packed.tile([P, POSITIONS], U8, align_bytes=64, name="scales_" + label)
            nc.vector.quantize_mx(out=codes[:].bitcast(FP8X4), scales=scales[:], in_=values)
            return codes, scales

        def multiply(g, a):
            g_in = g % UNIT_PASSES
            w_codes, w_scales = w_packed[unit_step[(a, g - g_in)]]
            x_codes, x_scales = x_packed[g]
            rows = slice(g_in * P, (g_in + 1) * P)
            nc.tensor.matmul_mx(
                out=acc[a][:],
                lhsT=w_codes[:, rows].bitcast(FP8X4),
                lhsT_scale=w_scales[:, rows],
                rhs=x_codes[:].bitcast(FP8X4),
                rhs_scale=x_scales[:],
                start=(g == 0),
                stop=(g == PASSES - 1),
            )

        for s in range(W_LEAD):
            load_w(s)
        for s in range(X_BUFS):
            load_x(s)
            load_w(s + W_LEAD)

        waiting = []
        for s in range(-FLIP_AHEAD, STEPS):
            if s + FLIP_AHEAD < STEPS:
                flip_w(s + FLIP_AHEAD)
            if s >= 0:
                group_x = regroup_x(s)
            if 0 <= s + COPY_AHEAD < STEPS:
                copy_w(s + COPY_AHEAD)
            if s >= 0:
                w_packed[s] = quantise(w_grouped[s][:], "w")
                x_packed[s] = quantise(group_x[:].rearrange("p n t -> p (n t)"), "x")
                a_new, first = unit_at[s]
                waiting.extend([(g, a_new) for g in range(first, min(first + UNIT_PASSES, s))])
                waiting.extend([(s, a) for a in range(ROW_TILES) if unit_step[(a, s - s % UNIT_PASSES)] <= s])
                count = len(waiting) if s >= STEPS - PERIODS[-1] else min(RUN_LIMIT, len(waiting))
                for g, a in waiting[0:count]:
                    multiply(g, a)
                waiting = waiting[count:]
                load_x(s + X_BUFS)
                load_w(s + X_BUFS + W_LEAD)

        def pool_2x2(pooled, a):
            nc.vector.tensor_reduce(
                out=pooled,
                in_=acc[a][:].rearrange("p (hp i wp j) -> p hp wp i j", hp=16, i=2, wp=8, j=2),
                axis=mybir.AxisListType.XY,
                op=mybir.AluOpType.max,
            )

        q_sb = results.tile([P, POSITIONS], F32)
        nc.scalar.copy(
            out=q_sb[:].rearrange("d (i p) -> d i p", i=4), in_=acc[0][:].rearrange("d (p i) -> d i p", i=4)
        )
        k_pooled = results.tile([P, 16, 8], F32)
        pool_2x2(k_pooled[:], 1)
        nc.sync.dma_start(out=out_1[0], in_=k_pooled[:].rearrange("p hp wp -> p (hp wp)"))
        q_flip = flip_pool.tile([P, 4, P], F32, name="bank")
        for b in range(4):
            nc.tensor.transpose(q_flip[:, b, :], q_sb[:, b * P : (b + 1) * P], ident[:])
        q_out = results.tile([P, 4, P], F32)
        nc.scalar.copy(out=q_out[:], in_=q_flip[:])
        nc.sync.dma_start(
            out=out_0[0].rearrange("(p i) d -> p (i d)", i=4), in_=q_out[:].rearrange("p i d -> p (i d)")
        )
        v_pooled = results.tile([P, 2, 16, 8], F32)
        pool_2x2(v_pooled[:, 0, :, :], 2)
        pool_2x2(v_pooled[:, 1, :, :], 3)
        nc.sync.dma_start(
            out=out_2[0].rearrange("(p a) m -> p (a m)", a=2),
            in_=v_pooled[:].rearrange("p a hp wp -> p (a hp wp)"),
        )
